import numpy as np
import ml_dtypes


def mxq(x, axis, fmt="e4m3"):
    dtype, down = {"e4m3": (ml_dtypes.float8_e4m3fn, 7), "e5m2": (ml_dtypes.float8_e5m2, 14)}[fmt]
    v = np.moveaxis(np.asarray(x, np.float32).astype(ml_dtypes.bfloat16).astype(np.float64), axis, -1)
    blocks = v.reshape(v.shape[:-1] + (-1, 32))
    amax = np.abs(blocks).max(-1, keepdims=True)
    byte = np.maximum(np.where(amax > 0, np.frexp(amax)[1] - 1 + 127, 0) - down, 1)
    scale = np.exp2(byte - 127.0)
    codes = (blocks / scale).astype(np.float32).astype(dtype).astype(np.float64)
    return np.moveaxis((codes * scale).reshape(v.shape), -1, axis)


WIDE = False


def mx_kscale(k):
    if not WIDE:
        return np.ones(k)
    levels = np.array([10, -10, 5, -5, 0])
    a = np.random.permutation(np.resize(levels, k // 512 * 4)).reshape(k // 512, 4)
    idx = np.arange(k)
    return np.exp2(a[idx // 512, idx % 128 // 32])


BF16 = ml_dtypes.bfloat16


def bf(x):
    return np.asarray(x, np.float32).astype(BF16)


def f64(x):
    return np.asarray(x).astype(np.float64)


B, T, D, M, C = 8, 512, 512, 2, 512
MD = M * D
LN_EPS = 1e-5


def setup_inputs():
    s, t = mx_kscale(T), mx_kscale(MD)
    sc = np.random.standard_normal((B, M, T, T)) * 2.0
    sc = np.where(np.tril(np.ones((T, T), dtype=bool)), sc, -np.inf)
    e = np.exp(sc - sc.max(-1, keepdims=True))
    attn = e / e.sum(-1, keepdims=True)
    return {"attn": bf(attn * s),
            "pz": bf(np.random.standard_normal((B, M, T, D)) / s[:, None] * t.reshape(M, 1, D)),
            "Wo": bf(np.random.standard_normal((D, MD)) * 2.0 / np.sqrt(MD) / t),
            "bo": bf(np.random.standard_normal(D) * 0.3),
            "x": bf(np.random.standard_normal((B, T, D))),
            "gamma": bf(1.0 + 0.1 * np.random.standard_normal(D)),
            "beta": bf(0.1 * np.random.standard_normal(D))}


def reference(attn, pz, Wo, bo, x, gamma, beta):
    a = f64(attn)
    pq = mxq(f64(pz), 2, "e4m3")
    rows = []
    for r in range(0, T, C):
        aq = mxq(a[:, :, r:r + C, :r + C], 3, "e4m3")
        rows.append(aq @ pq[:, :, :r + C, :])
    out = np.concatenate(rows, axis=2)
    cat = out.transpose(0, 2, 1, 3).reshape(B, T, MD)
    y = (mxq(cat, 2, "e4m3") @ mxq(f64(Wo), 1, "e4m3").T) + f64(bo)
    h = y + f64(x)
    mu = h.mean(-1, keepdims=True)
    var = h.var(-1, keepdims=True)
    return (h - mu) / np.sqrt(var + LN_EPS) * f64(gamma) + f64(beta)

@@ -1,0 +1,290 @@
+from contextlib import ExitStack
+
+import concourse.mybir as mybir
+from concourse.masks import make_identity
+
+F32 = mybir.dt.float32
+BF16 = mybir.dt.bfloat16
+U32 = mybir.dt.uint32
+U8 = mybir.dt.uint8
+FP8X4 = mybir.dt.float8_e4m3fn_x4
+ALU = mybir.AluOpType
+ACT = mybir.ActivationFunctionType
+
+P = 128
+PACK = 4
+B, M, T, D = 8, 2, 512, 512
+R = T // P
+UNITS = B * M
+PAIR = 2
+GROUPS = B * R // PAIR
+LN_EPS = 1e-5
+
+FLOPS = 2 * B * M * T * T * D + 2 * B * T * (M * D) * D
+
+PZ_GROUPS_VECTOR = 48
+PINNED = False
+BIAS_ON_GPSIMD = True
+LOAD_AHEAD = 5
+
+
+def tile_softmaxattention_pb_t_kernel(tc, attn, pz, Wo, bo, x, gamma, beta, out):
+    nc = tc.nc
+    with ExitStack() as stack:
+        consts = stack.enter_context(tc.tile_pool(name="consts", bufs=1))
+        loads = stack.enter_context(tc.tile_pool(name="loads", bufs=4))
+        grouped = stack.enter_context(tc.tile_pool(name="grouped", bufs=2))
+        mx = stack.enter_context(tc.tile_pool(name="mx", bufs=2))
+        rows = stack.enter_context(tc.tile_pool(name="rows", bufs=3))
+        stats = stack.enter_context(tc.tile_pool(name="stats", bufs=4))
+        psum_t = stack.enter_context(tc.psum_pool(name="psum_t", bufs=2))
+        psum_cat = stack.enter_context(tc.psum_pool(name="psum_cat", bufs=4))
+        psum_y = stack.enter_context(tc.psum_pool(name="psum_y", bufs=2))
+        if PINNED:
+            stack.enter_context(tc.manual_schedule())
+
+        attn_sb, pz_sb, x_sb = {}, {}, {}
+        t_banks, attn_grouped, pz_grouped, cat_grouped = {}, {}, {}, {}
+        attn_mx, pz_mx, cat_mx = {}, {}, {}
+        h, scaled, neg_mean, rstd = {}, {}, {}, {}
+
+        def load_unit(j):
+            b, m = divmod(j, M)
+            attn_sb[j] = loads.tile([P, R * T], BF16, name="attn_sb")
+            nc.sync.dma_start(out=attn_sb[j][:], in_=attn[b, m].rearrange("(p r) s -> p (r s)", r=R))
+            pz_sb[j] = loads.tile([P, PACK, D], BF16, name="pz_sb", bufs=5)
+            nc.sync.dma_start(
+                out=pz_sb[j][:].rearrange("p (u e) i -> p u (e i)", u=2),
+                in_=pz[b, m].rearrange("(u p e) i -> p u (e i)", u=2, e=2),
+            )
+            if m == 0:
+                x_sb[b] = loads.tile([P, R, D], BF16, name="x_sb")
+                nc.sync.dma_start(out=x_sb[b][:], in_=x[b].rearrange("(p r) o -> p r o", r=R))
+
+        def transpose_attn(j):
+            words = attn_sb[j][:].bitcast(F32).rearrange("p (r u w) -> p r u w", r=R, u=2)
+            t_banks[j] = []
+            for r0 in range(0, R, PAIR):
+                t_bank = psum_t.tile([P, PAIR, 2, P], F32, name="t_bank")
+                for r in range(PAIR):
+                    for u in range(2):
+                        nc.tensor.transpose(t_bank[:, r, u, :], words[:, r0 + r, u, :], ident_f32[:])
+                t_banks[j].append(t_bank)
+
+        def evacuate_attn(j):
+            attn_grouped[j] = grouped.tile([P, R * P * PACK], BF16, name="attn_grouped", align_bytes=64)
+            pairs = attn_grouped[j][:].bitcast(F32).rearrange("p (r t u) -> p r t u", r=R, u=2)
+            for k, t_bank in enumerate(t_banks[j]):
+                nc.scalar.copy(
+                    out=pairs[:, k * PAIR : (k + 1) * PAIR], in_=t_bank[:].rearrange("p r u t -> p r t u")
+                )
+
+        def pz_views(j):
+            src = pz_sb[j][:].rearrange("p j (g q) -> p g j q", q=4)
+            dst = pz_grouped[j][:].rearrange("p (g q) j -> p g j q", q=4)
+            return src, dst
+
+        def regroup_pz_scalar(j):
+            pz_grouped[j] = grouped.tile([P, D, PACK], BF16, name="pz_grouped", align_bytes=64)
+            src, dst = pz_views(j)
+            nc.scalar.copy(out=dst[:, PZ_GROUPS_VECTOR:], in_=src[:, PZ_GROUPS_VECTOR:])
+
+        def regroup_pz_vector(j):
+            src, dst = pz_views(j)
+            nc.vector.tensor_copy(out=dst[:, :PZ_GROUPS_VECTOR], in_=src[:, :PZ_GROUPS_VECTOR])
+
+        def quantise(name, values, bufs):
+            n = values.shape[1] // PACK
+            codes = mx.tile([P, n], U32, name=name + "_codes", align_bytes=64, bufs=bufs)
+            scales = mx.tile([P, n], U8, name=name + "_scales", align_bytes=64, bufs=bufs)
+            nc.vector.quantize_mx(out=codes[:].bitcast(FP8X4), scales=scales[:], in_=values)
+            return codes, scales
+
+        def quantise_front(j):
+            attn_mx[j] = quantise("attn", attn_grouped[j][:], 2)
+            pz_mx[j] = quantise("pz", pz_grouped[j][:].rearrange("p i j -> p (i j)"), 2)
+
+        def value_product(j):
+            attn_codes, attn_scales = attn_mx[j]
+            pz_codes, pz_scales = pz_mx[j]
+            cat_grouped[j] = grouped.tile([P, R, P, PACK], BF16, name="cat_grouped", align_bytes=64)
+            for r in range(R):
+                cat_bank = psum_cat.tile([P, PACK, P], F32, name="cat_bank")
+                for c in range(PACK):
+                    nc.tensor.matmul_mx(
+                        out=cat_bank[:, c, :],
+                        lhsT=pz_codes[:, c * P : (c + 1) * P].bitcast(FP8X4),
+                        lhsT_scale=pz_scales[:, c * P : (c + 1) * P],
+                        rhs=attn_codes[:, r * P : (r + 1) * P].bitcast(FP8X4),
+                        rhs_scale=attn_scales[:, r * P : (r + 1) * P],
+                        start=True,
+                        stop=True,
+                    )
+                nc.scalar.copy(out=cat_grouped[j][:, r], in_=cat_bank[:].rearrange("p c t -> p t c"))
+
+        def quantise_cat(j):
+            cat_mx[j] = quantise("cat", cat_grouped[j][:].rearrange("p r t c -> p (r t c)"), 4)
+
+        def add_bias(g):
+            b, k = divmod(g, R // PAIR)
+            h[g] = rows.tile([P, PAIR, D], F32, name="h")
+            engine = nc.gpsimd if BIAS_ON_GPSIMD else nc.vector
+            engine.tensor_tensor(
+                out=h[g][:],
+                in0=x_sb[b][:, k * PAIR : (k + 1) * PAIR, :],
+                in1=bo_all.unsqueeze(1).to_broadcast([P, PAIR, D]),
+                op=ALU.add,
+            )
+
+        def project(g):
+            b, k = divmod(g, R // PAIR)
+            row_sum = stats.tile([P, PAIR], F32, name="row_sum")
+            for i in range(PAIR):
+                r = k * PAIR + i
+                y_bank = psum_y.tile([P, D], F32, name="y_bank")
+                for m in range(M):
+                    cat_codes, cat_scales = cat_mx[b * M + m]
+                    nc.tensor.matmul_mx(
+                        out=y_bank[:],
+                        lhsT=cat_codes[:, r * P : (r + 1) * P].bitcast(FP8X4),
+                        lhsT_scale=cat_scales[:, r * P : (r + 1) * P],
+                        rhs=wo_codes[:, m * D : (m + 1) * D].bitcast(FP8X4),
+                        rhs_scale=wo_scales[:, m * D : (m + 1) * D],
+                        start=(m == 0),
+                        stop=(m == M - 1),
+                    )
+                nc.vector.scalar_tensor_tensor(
+                    out=h[g][:, i, :],
+                    in0=y_bank[:],
+                    scalar=1.0,
+                    in1=h[g][:, i, :],
+                    op0=ALU.mult,
+                    op1=ALU.add,
+                    accum_out=row_sum[:, i : i + 1],
+                )
+            neg_mean[g] = stats.tile([P, PAIR], F32, name="neg_mean")
+            nc.vector.tensor_scalar(
+                out=neg_mean[g][:], in0=row_sum[:], scalar1=-1.0 / D, scalar2=None, op0=ALU.mult
+            )
+
+        def scale_by_gamma(g):
+            scaled[g] = rows.tile([P, PAIR, D], F32, name="scaled")
+            for i in range(PAIR):
+                nc.vector.scalar_tensor_tensor(
+                    out=scaled[g][:, i, :],
+                    in0=h[g][:, i, :],
+                    scalar=neg_mean[g][:, i : i + 1],
+                    in1=gamma_all,
+                    op0=ALU.add,
+                    op1=ALU.mult,
+                )
+
+        def deviations(g):
+            squares = rows.tile([P, PAIR, D], BF16, name="squares", bufs=2)
+            dev_sum = stats.tile([P, PAIR], F32, name="dev_sum")
+            for i in range(PAIR):
+                nc.scalar.activation(
+                    out=squares[:, i, :],
+                    in_=h[g][:, i, :],
+                    func=ACT.Square,
+                    bias=neg_mean[g][:, i : i + 1],
+                    scale=1.0,
+                    accum_out=dev_sum[:, i : i + 1],
+                )
+            std = stats.tile([P, PAIR], F32, name="std")
+            nc.scalar.activation(out=std[:], in_=dev_sum[:], func=ACT.Sqrt, bias=eps[:], scale=1.0 / D)
+            rstd[g] = std
+
+        def finish(g):
+            b, k = divmod(g, R // PAIR)
+            inv = stats.tile([P, PAIR], F32, name="inv")
+            nc.vector.reciprocal(out=inv[:], in_=rstd[g][:])
+            for i in range(PAIR):
+                nc.vector.scalar_tensor_tensor(
+                    out=scaled[g][:, i, :],
+                    in0=scaled[g][:, i, :],
+                    scalar=inv[:, i : i + 1],
+                    in1=beta_all,
+                    op0=ALU.mult,
+                    op1=ALU.add,
+                )
+            nc.sync.dma_start(
+                out=out[b].rearrange("(p r) o -> p r o", r=R)[:, k * PAIR : (k + 1) * PAIR, :], in_=scaled[g][:]
+            )
+
+        load_unit(0)
+        load_unit(1)
+        wo_sb = consts.tile([P, D // P, M * D], BF16, name="wo_sb")
+        nc.sync.dma_start(out=wo_sb[:], in_=Wo.rearrange("(a q) j -> q a j", q=P))
+
+        ident_f32 = consts.tile([P, P], F32, name="ident_f32")
+        make_identity(nc, ident_f32[:])
+        ident_bf16 = consts.tile([P, P], BF16, name="ident_bf16")
+        make_identity(nc, ident_bf16[:])
+        eps = consts.tile([P, 1], F32, name="eps")
+        nc.vector.memset(eps[:], LN_EPS)
+
+        ones = consts.tile([P, P], BF16, name="ones")
+        nc.vector.memset(ones[:], 1.0)
+        vec_rows = consts.tile([P, 3, D], BF16, name="vec_rows")
+        nc.vector.memset(vec_rows[:], 0.0)
+        for v, vec in enumerate((bo, gamma, beta)):
+            nc.scalar.dma_start(out=vec_rows[0:1, v, :], in_=vec.rearrange("(one d) -> one d", one=1))
+        vec_all = consts.tile([P, 3, D], F32, name="vec_all")
+        for v in range(3):
+            vec_bank = psum_y.tile([P, D], F32, name="vec_bank", tag="y_bank")
+            nc.tensor.matmul(out=vec_bank[:], lhsT=ones[:], rhs=vec_rows[:, v, :], start=True, stop=True)
+            nc.vector.tensor_copy(out=vec_all[:, v, :], in_=vec_bank[:])
+        bo_all, gamma_all, beta_all = vec_all[:, 0, :], vec_all[:, 1, :], vec_all[:, 2, :]
+
+        wo_grouped = consts.tile([P, M, D, PACK], BF16, name="wo_grouped", align_bytes=64)
+        wo_codes = consts.tile([P, M * D], U32, name="wo_codes", align_bytes=64)
+        wo_scales = consts.tile([P, M * D], U8, name="wo_scales", align_bytes=64)
+
+        def prepare_wo():
+            for m in range(M):
+                for a0 in range(0, D // P, 2):
+                    wo_bank = psum_y.tile([P, 2, PACK, P], BF16, name="wo_bank", tag="y_bank")
+                    for a in range(2):
+                        for c in range(PACK):
+                            j0 = m * D + c * P
+                            nc.tensor.transpose(
+                                wo_bank[:, a, c, :], wo_sb[:, a0 + a, j0 : j0 + P], ident_bf16[:]
+                            )
+                    nc.vector.tensor_copy(
+                        out=wo_grouped[:, m, a0 * P : (a0 + 2) * P, :].rearrange("p (a o) c -> p a o c", a=2),
+                        in_=wo_bank[:].rearrange("p a c o -> p a o c"),
+                    )
+            nc.vector.quantize_mx(
+                out=wo_codes[:].bitcast(FP8X4),
+                scales=wo_scales[:],
+                in_=wo_grouped[:].rearrange("p m o c -> p (m o c)"),
+            )
+
+        for j in range(-3, UNITS + 2):
+            if 2 <= j + LOAD_AHEAD < UNITS:
+                load_unit(j + LOAD_AHEAD)
+            if 0 <= j < UNITS:
+                quantise_cat(j)
+            if 0 <= j + 2 < UNITS:
+                evacuate_attn(j + 2)
+            if 0 <= j + 3 < UNITS:
+                transpose_attn(j + 3)
+            if 0 <= j + 2 < UNITS:
+                regroup_pz_scalar(j + 2)
+            if 0 <= j + 1 < UNITS:
+                quantise_front(j + 1)
+            if 0 <= j - 1 < GROUPS:
+                project(j - 1)
+                scale_by_gamma(j - 1)
+                deviations(j - 1)
+            if 0 <= j + 1 < UNITS:
+                value_product(j + 1)
+            if 0 <= j + 2 < UNITS:
+                regroup_pz_vector(j + 2)
+            if 0 <= j + 1 < GROUPS:
+                add_bias(j + 1)
+            if j == -1:
+                prepare_wo()
+            if 0 <= j - 1 < GROUPS:
+                finish(j - 1)

@@ -38,7 +38,8 @@ def tile_softmaxattention_pb_t_kernel(tc, attn, pz, Wo, bo, x, gamma, beta, out)
         rows = stack.enter_context(tc.tile_pool(name="rows", bufs=3))
         stats = stack.enter_context(tc.tile_pool(name="stats", bufs=4))
         psum_t = stack.enter_context(tc.psum_pool(name="psum_t", bufs=2))
-        psum_cat = stack.enter_context(tc.psum_pool(name="psum_cat", bufs=4))
+        psum_cat = stack.enter_context(tc.psum_pool(name="psum_cat", bufs=2))
+        psum_consts = stack.enter_context(tc.psum_pool(name="psum_consts", bufs=1))
         psum_y = stack.enter_context(tc.psum_pool(name="psum_y", bufs=2))
         if PINNED:
             stack.enter_context(tc.manual_schedule())
@@ -230,12 +231,14 @@ def tile_softmaxattention_pb_t_kernel(tc, attn, pz, Wo, bo, x, gamma, beta, out)
         nc.vector.memset(vec_rows[:], 0.0)
         for v, vec in enumerate((bo, gamma, beta)):
             nc.scalar.dma_start(out=vec_rows[0:1, v, :], in_=vec.rearrange("(one d) -> one d", one=1))
-        vec_all = consts.tile([P, 3, D], F32, name="vec_all")
-        for v in range(3):
-            vec_bank = psum_y.tile([P, D], F32, name="vec_bank", tag="y_bank")
-            nc.tensor.matmul(out=vec_bank[:], lhsT=ones[:], rhs=vec_rows[:, v, :], start=True, stop=True)
-            nc.vector.tensor_copy(out=vec_all[:, v, :], in_=vec_bank[:])
-        bo_all, gamma_all, beta_all = vec_all[:, 0, :], vec_all[:, 1, :], vec_all[:, 2, :]
+        bo_bank = psum_y.tile([P, D], F32, name="bo_bank", tag="y_bank")
+        gamma_bank = psum_consts.tile([P, D], F32, name="gamma_bank")
+        beta_bank = psum_consts.tile([P, D], F32, name="beta_bank")
+        for v, bank in enumerate((bo_bank, gamma_bank, beta_bank)):
+            nc.tensor.matmul(out=bank[:], lhsT=ones[:], rhs=vec_rows[:, v, :], start=True, stop=True)
+        bo_sb = consts.tile([P, D], F32, name="bo_sb")
+        nc.vector.tensor_copy(out=bo_sb[:], in_=bo_bank[:])
+        bo_all, gamma_all, beta_all = bo_sb[:], gamma_bank[:], beta_bank[:]
 
         wo_grouped = consts.tile([P, M, D, PACK], BF16, name="wo_grouped", align_bytes=64)
         wo_codes = consts.tile([P, M * D], U32, name="wo_codes", align_bytes=64)

@@ -23,9 +23,6 @@ LN_EPS = 1e-5
 FLOPS = 2 * B * M * T * T * D + 2 * B * T * (M * D) * D
 
 PZ_GROUPS_VECTOR = 48
-PINNED = False
-BIAS_ON_GPSIMD = True
-LOAD_AHEAD = 5
 
 
 def tile_softmaxattention_pb_t_kernel(tc, attn, pz, Wo, bo, x, gamma, beta, out):
@@ -35,64 +32,64 @@ def tile_softmaxattention_pb_t_kernel(tc, attn, pz, Wo, bo, x, gamma, beta, out)
         loads = stack.enter_context(tc.tile_pool(name="loads", bufs=4))
         grouped = stack.enter_context(tc.tile_pool(name="grouped", bufs=2))
         mx = stack.enter_context(tc.tile_pool(name="mx", bufs=2))
-        rows = stack.enter_context(tc.tile_pool(name="rows", bufs=3))
-        stats = stack.enter_context(tc.tile_pool(name="stats", bufs=4))
+        rows = stack.enter_context(tc.tile_pool(name="rows", bufs=4))
+        stats = stack.enter_context(tc.tile_pool(name="stats", bufs=6))
         psum_t = stack.enter_context(tc.psum_pool(name="psum_t", bufs=2))
-        psum_cat = stack.enter_context(tc.psum_pool(name="psum_cat", bufs=2))
-        psum_consts = stack.enter_context(tc.psum_pool(name="psum_consts", bufs=1))
+        psum_cat = stack.enter_context(tc.psum_pool(name="psum_cat", bufs=3))
         psum_y = stack.enter_context(tc.psum_pool(name="psum_y", bufs=2))
-        if PINNED:
-            stack.enter_context(tc.manual_schedule())
+        psum_consts = stack.enter_context(tc.psum_pool(name="psum_consts", bufs=1))
+        stack.enter_context(tc.manual_schedule())
 
         attn_sb, pz_sb, x_sb = {}, {}, {}
         t_banks, attn_grouped, pz_grouped, cat_grouped = {}, {}, {}, {}
         attn_mx, pz_mx, cat_mx = {}, {}, {}
-        h, scaled, neg_mean, rstd = {}, {}, {}, {}
+        h, scaled, neg_mean, std = {}, {}, {}, {}
 
-        def load_unit(j):
-            b, m = divmod(j, M)
-            attn_sb[j] = loads.tile([P, R * T], BF16, name="attn_sb")
-            nc.sync.dma_start(out=attn_sb[j][:], in_=attn[b, m].rearrange("(p r) s -> p (r s)", r=R))
-            pz_sb[j] = loads.tile([P, PACK, D], BF16, name="pz_sb", bufs=5)
+        def load_unit(u):
+            b, m = divmod(u, M)
+            attn_sb[u] = loads.tile([P, R * T], BF16, name="attn_sb")
+            nc.sync.dma_start(out=attn_sb[u][:], in_=attn[b, m].rearrange("(p r) s -> p (r s)", r=R))
+            pz_sb[u] = loads.tile([P, PACK, D], BF16, name="pz_sb", bufs=5)
             nc.sync.dma_start(
-                out=pz_sb[j][:].rearrange("p (u e) i -> p u (e i)", u=2),
-                in_=pz[b, m].rearrange("(u p e) i -> p u (e i)", u=2, e=2),
+                out=pz_sb[u][:].rearrange("p (v e) i -> p v (e i)", v=2),
+                in_=pz[b, m].rearrange("(v p e) i -> p v (e i)", v=2, e=2),
             )
-            if m == 0:
-                x_sb[b] = loads.tile([P, R, D], BF16, name="x_sb")
-                nc.sync.dma_start(out=x_sb[b][:], in_=x[b].rearrange("(p r) o -> p r o", r=R))
 
-        def transpose_attn(j):
-            words = attn_sb[j][:].bitcast(F32).rearrange("p (r u w) -> p r u w", r=R, u=2)
-            t_banks[j] = []
+        def load_x(b):
+            x_sb[b] = loads.tile([P, R, D], BF16, name="x_sb", bufs=3)
+            nc.sync.dma_start(out=x_sb[b][:], in_=x[b].rearrange("(p r) o -> p r o", r=R))
+
+        def transpose_attn(u):
+            words = attn_sb[u][:].bitcast(F32).rearrange("p (r v w) -> p r v w", r=R, v=2)
+            t_banks[u] = []
             for r0 in range(0, R, PAIR):
                 t_bank = psum_t.tile([P, PAIR, 2, P], F32, name="t_bank")
                 for r in range(PAIR):
-                    for u in range(2):
-                        nc.tensor.transpose(t_bank[:, r, u, :], words[:, r0 + r, u, :], ident_f32[:])
-                t_banks[j].append(t_bank)
+                    for v in range(2):
+                        nc.tensor.transpose(t_bank[:, r, v, :], words[:, r0 + r, v, :], ident_f32[:])
+                t_banks[u].append(t_bank)
 
-        def evacuate_attn(j):
-            attn_grouped[j] = grouped.tile([P, R * P * PACK], BF16, name="attn_grouped", align_bytes=64)
-            pairs = attn_grouped[j][:].bitcast(F32).rearrange("p (r t u) -> p r t u", r=R, u=2)
-            for k, t_bank in enumerate(t_banks[j]):
+        def evacuate_attn(u):
+            attn_grouped[u] = grouped.tile([P, R * P * PACK], BF16, name="attn_grouped", align_bytes=64)
+            pairs = attn_grouped[u][:].bitcast(F32).rearrange("p (r t v) -> p r t v", r=R, v=2)
+            for k, t_bank in enumerate(t_banks[u]):
                 nc.scalar.copy(
-                    out=pairs[:, k * PAIR : (k + 1) * PAIR], in_=t_bank[:].rearrange("p r u t -> p r t u")
+                    out=pairs[:, k * PAIR : (k + 1) * PAIR], in_=t_bank[:].rearrange("p r v t -> p r t v")
                 )
 
-        def pz_views(j):
-            src = pz_sb[j][:].rearrange("p j (g q) -> p g j q", q=4)
-            dst = pz_grouped[j][:].rearrange("p (g q) j -> p g j q", q=4)
+        def pz_views(u):
+            src = pz_sb[u][:].rearrange("p j (g q) -> p g j q", q=4)
+            dst = pz_grouped[u][:].rearrange("p (g q) j -> p g j q", q=4)
             return src, dst
 
-        def regroup_pz_scalar(j):
-            pz_grouped[j] = grouped.tile([P, D, PACK], BF16, name="pz_grouped", align_bytes=64)
-            src, dst = pz_views(j)
-            nc.scalar.copy(out=dst[:, PZ_GROUPS_VECTOR:], in_=src[:, PZ_GROUPS_VECTOR:])
-
-        def regroup_pz_vector(j):
-            src, dst = pz_views(j)
+        def regroup_pz_vector(u):
+            pz_grouped[u] = grouped.tile([P, D, PACK], BF16, name="pz_grouped", align_bytes=64)
+            src, dst = pz_views(u)
             nc.vector.tensor_copy(out=dst[:, :PZ_GROUPS_VECTOR], in_=src[:, :PZ_GROUPS_VECTOR])
+
+        def regroup_pz_scalar(u):
+            src, dst = pz_views(u)
+            nc.scalar.copy(out=dst[:, PZ_GROUPS_VECTOR:], in_=src[:, PZ_GROUPS_VECTOR:])
 
         def quantise(name, values, bufs):
             n = values.shape[1] // PACK
@@ -101,14 +98,14 @@ def tile_softmaxattention_pb_t_kernel(tc, attn, pz, Wo, bo, x, gamma, beta, out)
             nc.vector.quantize_mx(out=codes[:].bitcast(FP8X4), scales=scales[:], in_=values)
             return codes, scales
 
-        def quantise_front(j):
-            attn_mx[j] = quantise("attn", attn_grouped[j][:], 2)
-            pz_mx[j] = quantise("pz", pz_grouped[j][:].rearrange("p i j -> p (i j)"), 2)
+        def quantise_front(u):
+            attn_mx[u] = quantise("attn", attn_grouped[u][:], 2)
+            pz_mx[u] = quantise("pz", pz_grouped[u][:].rearrange("p i j -> p (i j)"), 2)
 
-        def value_product(j):
-            attn_codes, attn_scales = attn_mx[j]
-            pz_codes, pz_scales = pz_mx[j]
-            cat_grouped[j] = grouped.tile([P, R, P, PACK], BF16, name="cat_grouped", align_bytes=64)
+        def value_product(u):
+            attn_codes, attn_scales = attn_mx[u]
+            pz_codes, pz_scales = pz_mx[u]
+            cat_grouped[u] = grouped.tile([P, R, P, PACK], BF16, name="cat_grouped", align_bytes=64)
             for r in range(R):
                 cat_bank = psum_cat.tile([P, PACK, P], F32, name="cat_bank")
                 for c in range(PACK):
@@ -121,21 +118,16 @@ def tile_softmaxattention_pb_t_kernel(tc, attn, pz, Wo, bo, x, gamma, beta, out)
                         start=True,
                         stop=True,
                     )
-                nc.scalar.copy(out=cat_grouped[j][:, r], in_=cat_bank[:].rearrange("p c t -> p t c"))
+                nc.scalar.copy(out=cat_grouped[u][:, r], in_=cat_bank[:].rearrange("p c t -> p t c"))
 
-        def quantise_cat(j):
-            cat_mx[j] = quantise("cat", cat_grouped[j][:].rearrange("p r t c -> p (r t c)"), 4)
+        def quantise_cat(u):
+            cat_mx[u] = quantise("cat", cat_grouped[u][:].rearrange("p r t c -> p (r t c)"), 5)
 
         def add_bias(g):
             b, k = divmod(g, R // PAIR)
-            h[g] = rows.tile([P, PAIR, D], F32, name="h")
-            engine = nc.gpsimd if BIAS_ON_GPSIMD else nc.vector
-            engine.tensor_tensor(
-                out=h[g][:],
-                in0=x_sb[b][:, k * PAIR : (k + 1) * PAIR, :],
-                in1=bo_all.unsqueeze(1).to_broadcast([P, PAIR, D]),
-                op=ALU.add,
-            )
+            h[g] = rows.tile([P, PAIR, D], F32, name="h", bufs=5)
+            for i in range(PAIR):
+                nc.gpsimd.tensor_tensor(out=h[g][:, i, :], in0=x_sb[b][:, k * PAIR + i, :], in1=bo_all[:], op=ALU.add)
 
         def project(g):
             b, k = divmod(g, R // PAIR)
@@ -167,8 +159,6 @@ def tile_softmaxattention_pb_t_kernel(tc, attn, pz, Wo, bo, x, gamma, beta, out)
             nc.vector.tensor_scalar(
                 out=neg_mean[g][:], in0=row_sum[:], scalar1=-1.0 / D, scalar2=None, op0=ALU.mult
             )
-
-        def scale_by_gamma(g):
             scaled[g] = rows.tile([P, PAIR, D], F32, name="scaled")
             for i in range(PAIR):
                 nc.vector.scalar_tensor_tensor(
@@ -192,19 +182,18 @@ def tile_softmaxattention_pb_t_kernel(tc, attn, pz, Wo, bo, x, gamma, beta, out)
                     scale=1.0,
                     accum_out=dev_sum[:, i : i + 1],
                 )
-            std = stats.tile([P, PAIR], F32, name="std")
-            nc.scalar.activation(out=std[:], in_=dev_sum[:], func=ACT.Sqrt, bias=eps[:], scale=1.0 / D)
-            rstd[g] = std
+            std[g] = stats.tile([P, PAIR], F32, name="std")
+            nc.scalar.activation(out=std[g][:], in_=dev_sum[:], func=ACT.Sqrt, bias=eps[:], scale=1.0 / D)
 
         def finish(g):
             b, k = divmod(g, R // PAIR)
-            inv = stats.tile([P, PAIR], F32, name="inv")
-            nc.vector.reciprocal(out=inv[:], in_=rstd[g][:])
+            rstd = stats.tile([P, PAIR], F32, name="rstd")
+            nc.vector.reciprocal(out=rstd[:], in_=std[g][:])
             for i in range(PAIR):
                 nc.vector.scalar_tensor_tensor(
                     out=scaled[g][:, i, :],
                     in0=scaled[g][:, i, :],
-                    scalar=inv[:, i : i + 1],
+                    scalar=rstd[:, i : i + 1],
                     in1=beta_all,
                     op0=ALU.mult,
                     op1=ALU.add,
@@ -213,36 +202,8 @@ def tile_softmaxattention_pb_t_kernel(tc, attn, pz, Wo, bo, x, gamma, beta, out)
                 out=out[b].rearrange("(p r) o -> p r o", r=R)[:, k * PAIR : (k + 1) * PAIR, :], in_=scaled[g][:]
             )
 
-        load_unit(0)
-        load_unit(1)
-        wo_sb = consts.tile([P, D // P, M * D], BF16, name="wo_sb")
-        nc.sync.dma_start(out=wo_sb[:], in_=Wo.rearrange("(a q) j -> q a j", q=P))
-
-        ident_f32 = consts.tile([P, P], F32, name="ident_f32")
-        make_identity(nc, ident_f32[:])
-        ident_bf16 = consts.tile([P, P], BF16, name="ident_bf16")
-        make_identity(nc, ident_bf16[:])
-        eps = consts.tile([P, 1], F32, name="eps")
-        nc.vector.memset(eps[:], LN_EPS)
-
-        ones = consts.tile([P, P], BF16, name="ones")
-        nc.vector.memset(ones[:], 1.0)
-        vec_rows = consts.tile([P, 3, D], BF16, name="vec_rows")
-        nc.vector.memset(vec_rows[:], 0.0)
-        for v, vec in enumerate((bo, gamma, beta)):
-            nc.scalar.dma_start(out=vec_rows[0:1, v, :], in_=vec.rearrange("(one d) -> one d", one=1))
-        bo_bank = psum_y.tile([P, D], F32, name="bo_bank", tag="y_bank")
-        gamma_bank = psum_consts.tile([P, D], F32, name="gamma_bank")
-        beta_bank = psum_consts.tile([P, D], F32, name="beta_bank")
-        for v, bank in enumerate((bo_bank, gamma_bank, beta_bank)):
-            nc.tensor.matmul(out=bank[:], lhsT=ones[:], rhs=vec_rows[:, v, :], start=True, stop=True)
-        bo_sb = consts.tile([P, D], F32, name="bo_sb")
-        nc.vector.tensor_copy(out=bo_sb[:], in_=bo_bank[:])
-        bo_all, gamma_all, beta_all = bo_sb[:], gamma_bank[:], beta_bank[:]
-
-        wo_grouped = consts.tile([P, M, D, PACK], BF16, name="wo_grouped", align_bytes=64)
-        wo_codes = consts.tile([P, M * D], U32, name="wo_codes", align_bytes=64)
-        wo_scales = consts.tile([P, M * D], U8, name="wo_scales", align_bytes=64)
+        def load_wo():
+            nc.sync.dma_start(out=wo_sb[:], in_=Wo.rearrange("(a q) j -> q a j", q=P))
 
         def prepare_wo():
             for m in range(M):
@@ -264,30 +225,55 @@ def tile_softmaxattention_pb_t_kernel(tc, attn, pz, Wo, bo, x, gamma, beta, out)
                 in_=wo_grouped[:].rearrange("p m o c -> p (m o c)"),
             )
 
-        for j in range(-3, UNITS + 2):
-            if 2 <= j + LOAD_AHEAD < UNITS:
-                load_unit(j + LOAD_AHEAD)
-            if 0 <= j < UNITS:
-                quantise_cat(j)
-            if 0 <= j + 2 < UNITS:
-                evacuate_attn(j + 2)
-            if 0 <= j + 3 < UNITS:
-                transpose_attn(j + 3)
-            if 0 <= j + 2 < UNITS:
-                regroup_pz_scalar(j + 2)
-            if 0 <= j + 1 < UNITS:
-                quantise_front(j + 1)
-            if 0 <= j - 1 < GROUPS:
-                project(j - 1)
-                scale_by_gamma(j - 1)
-                deviations(j - 1)
-            if 0 <= j + 1 < UNITS:
-                value_product(j + 1)
-            if 0 <= j + 2 < UNITS:
-                regroup_pz_vector(j + 2)
-            if 0 <= j + 1 < GROUPS:
-                add_bias(j + 1)
-            if j == -1:
+        def when(k, count, phase):
+            if 0 <= k < count:
+                phase(k)
+
+        load_unit(0)
+        load_unit(1)
+        wo_sb = consts.tile([P, D // P, M * D], BF16, name="wo_sb")
+        wo_grouped = consts.tile([P, M, D, PACK], BF16, name="wo_grouped", align_bytes=64)
+        wo_codes = consts.tile([P, M * D], U32, name="wo_codes", align_bytes=64)
+        wo_scales = consts.tile([P, M * D], U8, name="wo_scales", align_bytes=64)
+
+        ident_f32 = consts.tile([P, P], F32, name="ident_f32")
+        make_identity(nc, ident_f32[:])
+        ident_bf16 = consts.tile([P, P], BF16, name="ident_bf16")
+        make_identity(nc, ident_bf16[:])
+        eps = consts.tile([P, 1], F32, name="eps")
+        nc.vector.memset(eps[:], LN_EPS)
+
+        ones = consts.tile([P, P], BF16, name="ones")
+        nc.vector.memset(ones[:], 1.0)
+        vec_rows = consts.tile([P, 3, D], BF16, name="vec_rows")
+        nc.vector.memset(vec_rows[:], 0.0)
+        for v, vec in enumerate((bo, gamma, beta)):
+            nc.scalar.dma_start(out=vec_rows[0:1, v, :], in_=vec.rearrange("(one d) -> one d", one=1))
+        bo_bank = psum_y.tile([P, D], F32, name="bo_bank", tag="y_bank")
+        nc.tensor.matmul(out=bo_bank[:], lhsT=ones[:], rhs=vec_rows[:, 0, :], start=True, stop=True)
+        bo_all = consts.tile([P, D], F32, name="bo_all")
+        nc.vector.tensor_copy(out=bo_all[:], in_=bo_bank[:])
+        affine_bank = psum_consts.tile([P, 2, D], BF16, name="affine_bank")
+        for v in range(2):
+            nc.tensor.matmul(out=affine_bank[:, v, :], lhsT=ones[:], rhs=vec_rows[:, 1 + v, :], start=True, stop=True)
+        gamma_all, beta_all = affine_bank[:, 0, :], affine_bank[:, 1, :]
+
+        for i in range(-8, GROUPS):
+            when(i + 10, UNITS, load_unit)
+            if (i + 7) % 2 == 0:
+                when((i + 7) // 2, B, load_x)
+            if i == -7:
+                load_wo()
+            when(i + 4, UNITS, quantise_cat)
+            when(i + 6, UNITS, quantise_front)
+            when(i + 7, UNITS, regroup_pz_vector)
+            if i == -4:
                 prepare_wo()
-            if 0 <= j - 1 < GROUPS:
-                finish(j - 1)
+            when(i, GROUPS, finish)
+            when(i + 2, GROUPS, project)
+            when(i + 1, GROUPS, deviations)
+            when(i + 7, UNITS, evacuate_attn)
+            when(i + 7, UNITS, regroup_pz_scalar)
+            when(i + 5, UNITS, value_product)
+            when(i + 8, UNITS, transpose_attn)
+            when(i + 4, GROUPS, add_bias)

@@ -22,7 +22,7 @@ LN_EPS = 1e-5
 
 FLOPS = 2 * B * M * T * T * D + 2 * B * T * (M * D) * D
 
-PZ_GROUPS_VECTOR = 48
+PZ_GROUPS_VECTOR = 64
 
 
 def tile_softmaxattention_pb_t_kernel(tc, attn, pz, Wo, bo, x, gamma, beta, out):
@@ -121,11 +121,11 @@ def tile_softmaxattention_pb_t_kernel(tc, attn, pz, Wo, bo, x, gamma, beta, out)
                 nc.scalar.copy(out=cat_grouped[u][:, r], in_=cat_bank[:].rearrange("p c t -> p t c"))
 
         def quantise_cat(u):
-            cat_mx[u] = quantise("cat", cat_grouped[u][:].rearrange("p r t c -> p (r t c)"), 5)
+            cat_mx[u] = quantise("cat", cat_grouped[u][:].rearrange("p r t c -> p (r t c)"), 4)
 
         def add_bias(g):
             b, k = divmod(g, R // PAIR)
-            h[g] = rows.tile([P, PAIR, D], F32, name="h", bufs=5)
+            h[g] = rows.tile([P, PAIR, D], F32, name="h")
             for i in range(PAIR):
                 nc.gpsimd.tensor_tensor(out=h[g][:, i, :], in0=x_sb[b][:, k * PAIR + i, :], in1=bo_all[:], op=ALU.add)
 
@@ -159,7 +159,7 @@ def tile_softmaxattention_pb_t_kernel(tc, attn, pz, Wo, bo, x, gamma, beta, out)
             nc.vector.tensor_scalar(
                 out=neg_mean[g][:], in0=row_sum[:], scalar1=-1.0 / D, scalar2=None, op0=ALU.mult
             )
-            scaled[g] = rows.tile([P, PAIR, D], F32, name="scaled")
+            scaled[g] = rows.tile([P, PAIR, D], F32, name="scaled", bufs=5)
             for i in range(PAIR):
                 nc.vector.scalar_tensor_tensor(
                     out=scaled[g][:, i, :],
@@ -205,24 +205,21 @@ def tile_softmaxattention_pb_t_kernel(tc, attn, pz, Wo, bo, x, gamma, beta, out)
         def load_wo():
             nc.sync.dma_start(out=wo_sb[:], in_=Wo.rearrange("(a q) j -> q a j", q=P))
 
-        def prepare_wo():
-            for m in range(M):
-                for a0 in range(0, D // P, 2):
-                    wo_bank = psum_y.tile([P, 2, PACK, P], BF16, name="wo_bank", tag="y_bank")
-                    for a in range(2):
-                        for c in range(PACK):
-                            j0 = m * D + c * P
-                            nc.tensor.transpose(
-                                wo_bank[:, a, c, :], wo_sb[:, a0 + a, j0 : j0 + P], ident_bf16[:]
-                            )
-                    nc.vector.tensor_copy(
-                        out=wo_grouped[:, m, a0 * P : (a0 + 2) * P, :].rearrange("p (a o) c -> p a o c", a=2),
-                        in_=wo_bank[:].rearrange("p a c o -> p a o c"),
-                    )
+        def prepare_wo(m):
+            for a0 in range(0, D // P, 2):
+                wo_bank = psum_y.tile([P, 2, PACK, P], BF16, name="wo_bank", tag="y_bank")
+                for a in range(2):
+                    for c in range(PACK):
+                        j0 = m * D + c * P
+                        nc.tensor.transpose(wo_bank[:, a, c, :], wo_sb[:, a0 + a, j0 : j0 + P], ident_bf16[:])
+                nc.vector.tensor_copy(
+                    out=wo_grouped[:, m, a0 * P : (a0 + 2) * P, :].rearrange("p (a o) c -> p a o c", a=2),
+                    in_=wo_bank[:].rearrange("p a c o -> p a o c"),
+                )
             nc.vector.quantize_mx(
-                out=wo_codes[:].bitcast(FP8X4),
-                scales=wo_scales[:],
-                in_=wo_grouped[:].rearrange("p m o c -> p (m o c)"),
+                out=wo_codes[:, m * D : (m + 1) * D].bitcast(FP8X4),
+                scales=wo_scales[:, m * D : (m + 1) * D],
+                in_=wo_grouped[:, m].rearrange("p o c -> p (o c)"),
             )
 
         def when(k, count, phase):
@@ -232,6 +229,7 @@ def tile_softmaxattention_pb_t_kernel(tc, attn, pz, Wo, bo, x, gamma, beta, out)
         load_unit(0)
         load_unit(1)
         wo_sb = consts.tile([P, D // P, M * D], BF16, name="wo_sb")
+        load_wo()
         wo_grouped = consts.tile([P, M, D, PACK], BF16, name="wo_grouped", align_bytes=64)
         wo_codes = consts.tile([P, M * D], U32, name="wo_codes", align_bytes=64)
         wo_scales = consts.tile([P, M * D], U8, name="wo_scales", align_bytes=64)
@@ -249,31 +247,34 @@ def tile_softmaxattention_pb_t_kernel(tc, attn, pz, Wo, bo, x, gamma, beta, out)
         nc.vector.memset(vec_rows[:], 0.0)
         for v, vec in enumerate((bo, gamma, beta)):
             nc.scalar.dma_start(out=vec_rows[0:1, v, :], in_=vec.rearrange("(one d) -> one d", one=1))
-        bo_bank = psum_y.tile([P, D], F32, name="bo_bank", tag="y_bank")
-        nc.tensor.matmul(out=bo_bank[:], lhsT=ones[:], rhs=vec_rows[:, 0, :], start=True, stop=True)
         bo_all = consts.tile([P, D], F32, name="bo_all")
-        nc.vector.tensor_copy(out=bo_all[:], in_=bo_bank[:])
         affine_bank = psum_consts.tile([P, 2, D], BF16, name="affine_bank")
-        for v in range(2):
-            nc.tensor.matmul(out=affine_bank[:, v, :], lhsT=ones[:], rhs=vec_rows[:, 1 + v, :], start=True, stop=True)
         gamma_all, beta_all = affine_bank[:, 0, :], affine_bank[:, 1, :]
 
-        for i in range(-8, GROUPS):
-            when(i + 10, UNITS, load_unit)
-            if (i + 7) % 2 == 0:
-                when((i + 7) // 2, B, load_x)
-            if i == -7:
-                load_wo()
-            when(i + 4, UNITS, quantise_cat)
-            when(i + 6, UNITS, quantise_front)
-            when(i + 7, UNITS, regroup_pz_vector)
-            if i == -4:
-                prepare_wo()
-            when(i, GROUPS, finish)
-            when(i + 2, GROUPS, project)
-            when(i + 1, GROUPS, deviations)
-            when(i + 7, UNITS, evacuate_attn)
-            when(i + 7, UNITS, regroup_pz_scalar)
-            when(i + 5, UNITS, value_product)
-            when(i + 8, UNITS, transpose_attn)
-            when(i + 4, GROUPS, add_bias)
+        def broadcast_vectors():
+            bo_bank = psum_y.tile([P, D], F32, name="bo_bank", tag="y_bank")
+            nc.tensor.matmul(out=bo_bank[:], lhsT=ones[:], rhs=vec_rows[:, 0, :], start=True, stop=True)
+            nc.vector.tensor_copy(out=bo_all[:], in_=bo_bank[:])
+            for v in range(2):
+                nc.tensor.matmul(
+                    out=affine_bank[:, v, :], lhsT=ones[:], rhs=vec_rows[:, 1 + v, :], start=True, stop=True
+                )
+
+        for j in range(-3, GROUPS + 3):
+            when(j + 5, UNITS, load_unit)
+            if (j + 3) % 2 == 0:
+                when((j + 3) // 2, B, load_x)
+            when(j - 2, GROUPS, deviations)
+            when(j + 1, UNITS, quantise_front)
+            when(j + 2, UNITS, regroup_pz_vector)
+            when(j, UNITS, quantise_cat)
+            when(j + 1, M, prepare_wo)
+            when(j - 3, GROUPS, finish)
+            when(j - 1, GROUPS, project)
+            when(j + 2, UNITS, evacuate_attn)
+            when(j + 2, UNITS, regroup_pz_scalar)
+            when(j + 1, UNITS, value_product)
+            when(j + 3, UNITS, transpose_attn)
+            if j == -2:
+                broadcast_vectors()
+            when(j + 1, GROUPS, add_bias)

@@ -22,18 +22,19 @@ LN_EPS = 1e-5
 
 FLOPS = 2 * B * M * T * T * D + 2 * B * T * (M * D) * D
 
-PZ_GROUPS_VECTOR = 64
+PZ_GROUPS_GPSIMD = 80
+PZ_PIECES = 2
 
 
 def tile_softmaxattention_pb_t_kernel(tc, attn, pz, Wo, bo, x, gamma, beta, out):
     nc = tc.nc
     with ExitStack() as stack:
         consts = stack.enter_context(tc.tile_pool(name="consts", bufs=1))
-        loads = stack.enter_context(tc.tile_pool(name="loads", bufs=4))
-        grouped = stack.enter_context(tc.tile_pool(name="grouped", bufs=2))
+        loads = stack.enter_context(tc.tile_pool(name="loads", bufs=5))
+        grouped = stack.enter_context(tc.tile_pool(name="grouped", bufs=3))
         mx = stack.enter_context(tc.tile_pool(name="mx", bufs=2))
         rows = stack.enter_context(tc.tile_pool(name="rows", bufs=4))
-        stats = stack.enter_context(tc.tile_pool(name="stats", bufs=6))
+        stats = stack.enter_context(tc.tile_pool(name="stats", bufs=8))
         psum_t = stack.enter_context(tc.psum_pool(name="psum_t", bufs=2))
         psum_cat = stack.enter_context(tc.psum_pool(name="psum_cat", bufs=3))
         psum_y = stack.enter_context(tc.psum_pool(name="psum_y", bufs=2))
@@ -43,7 +44,7 @@ def tile_softmaxattention_pb_t_kernel(tc, attn, pz, Wo, bo, x, gamma, beta, out)
         attn_sb, pz_sb, x_sb = {}, {}, {}
         t_banks, attn_grouped, pz_grouped, cat_grouped = {}, {}, {}, {}
         attn_mx, pz_mx, cat_mx = {}, {}, {}
-        h, scaled, neg_mean, std = {}, {}, {}, {}
+        h, scaled, row_sum, neg_mean, rstd, y_banks = {}, {}, {}, {}, {}, {}
 
         def load_unit(u):
             b, m = divmod(u, M)
@@ -82,14 +83,22 @@ def tile_softmaxattention_pb_t_kernel(tc, attn, pz, Wo, bo, x, gamma, beta, out)
             dst = pz_grouped[u][:].rearrange("p (g q) j -> p g j q", q=4)
             return src, dst
 
-        def regroup_pz_vector(u):
+        def regroup_pz_gpsimd(u):
             pz_grouped[u] = grouped.tile([P, D, PACK], BF16, name="pz_grouped", align_bytes=64)
-            src, dst = pz_views(u)
-            nc.vector.tensor_copy(out=dst[:, :PZ_GROUPS_VECTOR], in_=src[:, :PZ_GROUPS_VECTOR])
+            step = PZ_GROUPS_GPSIMD * 4 // PZ_PIECES
+            for c0 in range(0, PZ_GROUPS_GPSIMD * 4, step):
+                nc.gpsimd.tensor_scalar(
+                    out=pz_grouped[u][:, c0 : c0 + step, :],
+                    in0=pz_sb[u][:, :, c0 : c0 + step].rearrange("p j i -> p i j"),
+                    scalar1=1.0,
+                    scalar2=0.0,
+                    op0=ALU.mult,
+                    op1=ALU.add,
+                )
 
         def regroup_pz_scalar(u):
             src, dst = pz_views(u)
-            nc.scalar.copy(out=dst[:, PZ_GROUPS_VECTOR:], in_=src[:, PZ_GROUPS_VECTOR:])
+            nc.scalar.copy(out=dst[:, PZ_GROUPS_GPSIMD:], in_=src[:, PZ_GROUPS_GPSIMD:])
 
         def quantise(name, values, bufs):
             n = values.shape[1] // PACK
@@ -125,20 +134,19 @@ def tile_softmaxattention_pb_t_kernel(tc, attn, pz, Wo, bo, x, gamma, beta, out)
 
         def add_bias(g):
             b, k = divmod(g, R // PAIR)
-            h[g] = rows.tile([P, PAIR, D], F32, name="h")
             for i in range(PAIR):
-                nc.gpsimd.tensor_tensor(out=h[g][:, i, :], in0=x_sb[b][:, k * PAIR + i, :], in1=bo_all[:], op=ALU.add)
+                h[g, i] = rows.tile([P, D], F32, name="h", bufs=2 * PAIR)
+                nc.gpsimd.tensor_tensor(out=h[g, i][:], in0=x_sb[b][:, k * PAIR + i, :], in1=bo_all[:], op=ALU.add)
 
         def project(g):
             b, k = divmod(g, R // PAIR)
-            row_sum = stats.tile([P, PAIR], F32, name="row_sum")
             for i in range(PAIR):
                 r = k * PAIR + i
-                y_bank = psum_y.tile([P, D], F32, name="y_bank")
+                y_banks[g, i] = psum_y.tile([P, D], F32, name="y_bank")
                 for m in range(M):
                     cat_codes, cat_scales = cat_mx[b * M + m]
                     nc.tensor.matmul_mx(
-                        out=y_bank[:],
+                        out=y_banks[g, i][:],
                         lhsT=cat_codes[:, r * P : (r + 1) * P].bitcast(FP8X4),
                         lhsT_scale=cat_scales[:, r * P : (r + 1) * P],
                         rhs=wo_codes[:, m * D : (m + 1) * D].bitcast(FP8X4),
@@ -146,54 +154,58 @@ def tile_softmaxattention_pb_t_kernel(tc, attn, pz, Wo, bo, x, gamma, beta, out)
                         start=(m == 0),
                         stop=(m == M - 1),
                     )
+
+        def residual(g):
+            row_sum[g] = stats.tile([P, PAIR], F32, name="row_sum")
+            for i in range(PAIR):
                 nc.vector.scalar_tensor_tensor(
-                    out=h[g][:, i, :],
-                    in0=y_bank[:],
+                    out=h[g, i][:],
+                    in0=y_banks[g, i][:],
                     scalar=1.0,
-                    in1=h[g][:, i, :],
+                    in1=h[g, i][:],
                     op0=ALU.mult,
                     op1=ALU.add,
-                    accum_out=row_sum[:, i : i + 1],
+                    accum_out=row_sum[g][:, i : i + 1],
                 )
+
+        def deviations(g):
             neg_mean[g] = stats.tile([P, PAIR], F32, name="neg_mean")
-            nc.vector.tensor_scalar(
-                out=neg_mean[g][:], in0=row_sum[:], scalar1=-1.0 / D, scalar2=None, op0=ALU.mult
+            nc.scalar.activation(out=neg_mean[g][:], in_=row_sum[g][:], func=ACT.Copy, scale=-1.0 / D)
+            squares = rows.tile([P, PAIR, D], BF16, name="squares", bufs=2)
+            dev_sum = stats.tile([P, PAIR], F32, name="dev_sum")
+            for i in range(PAIR):
+                nc.scalar.activation(
+                    out=squares[:, i, :],
+                    in_=h[g, i][:],
+                    func=ACT.Square,
+                    bias=neg_mean[g][:, i : i + 1],
+                    scale=1.0,
+                    accum_out=dev_sum[:, i : i + 1],
+                )
+            rstd[g] = stats.tile([P, PAIR], F32, name="rstd")
+            nc.scalar.activation(
+                out=rstd[g][:], in_=dev_sum[:], func=ACT.Abs_reciprocal_sqrt, bias=eps[:], scale=1.0 / D
             )
-            scaled[g] = rows.tile([P, PAIR, D], F32, name="scaled", bufs=5)
+
+        def centre(g):
+            scaled[g] = rows.tile([P, PAIR, D], F32, name="scaled", bufs=4)
             for i in range(PAIR):
                 nc.vector.scalar_tensor_tensor(
                     out=scaled[g][:, i, :],
-                    in0=h[g][:, i, :],
+                    in0=h[g, i][:],
                     scalar=neg_mean[g][:, i : i + 1],
                     in1=gamma_all,
                     op0=ALU.add,
                     op1=ALU.mult,
                 )
 
-        def deviations(g):
-            squares = rows.tile([P, PAIR, D], BF16, name="squares", bufs=2)
-            dev_sum = stats.tile([P, PAIR], F32, name="dev_sum")
-            for i in range(PAIR):
-                nc.scalar.activation(
-                    out=squares[:, i, :],
-                    in_=h[g][:, i, :],
-                    func=ACT.Square,
-                    bias=neg_mean[g][:, i : i + 1],
-                    scale=1.0,
-                    accum_out=dev_sum[:, i : i + 1],
-                )
-            std[g] = stats.tile([P, PAIR], F32, name="std")
-            nc.scalar.activation(out=std[g][:], in_=dev_sum[:], func=ACT.Sqrt, bias=eps[:], scale=1.0 / D)
-
         def finish(g):
             b, k = divmod(g, R // PAIR)
-            rstd = stats.tile([P, PAIR], F32, name="rstd")
-            nc.vector.reciprocal(out=rstd[:], in_=std[g][:])
             for i in range(PAIR):
                 nc.vector.scalar_tensor_tensor(
                     out=scaled[g][:, i, :],
                     in0=scaled[g][:, i, :],
-                    scalar=rstd[:, i : i + 1],
+                    scalar=rstd[g][:, i : i + 1],
                     in1=beta_all,
                     op0=ALU.mult,
                     op1=ALU.add,
@@ -221,6 +233,10 @@ def tile_softmaxattention_pb_t_kernel(tc, attn, pz, Wo, bo, x, gamma, beta, out)
                 scales=wo_scales[:, m * D : (m + 1) * D],
                 in_=wo_grouped[:, m].rearrange("p o c -> p (o c)"),
             )
+
+        def load_late_unit(u):
+            if u >= 2:
+                load_unit(u)
 
         def when(k, count, phase):
             if 0 <= k < count:
@@ -260,21 +276,23 @@ def tile_softmaxattention_pb_t_kernel(tc, attn, pz, Wo, bo, x, gamma, beta, out)
                     out=affine_bank[:, v, :], lhsT=ones[:], rhs=vec_rows[:, 1 + v, :], start=True, stop=True
                 )
 
-        for j in range(-3, GROUPS + 3):
-            when(j + 5, UNITS, load_unit)
-            if (j + 3) % 2 == 0:
-                when((j + 3) // 2, B, load_x)
-            when(j - 2, GROUPS, deviations)
-            when(j + 1, UNITS, quantise_front)
-            when(j + 2, UNITS, regroup_pz_vector)
-            when(j, UNITS, quantise_cat)
-            when(j + 1, M, prepare_wo)
-            when(j - 3, GROUPS, finish)
-            when(j - 1, GROUPS, project)
+        for j in range(-2, GROUPS + 5):
+            when(j + 4, UNITS, load_late_unit)
+            if (j + 2) % 2 == 0:
+                when((j + 2) // 2, B, load_x)
+            when(j - 3, GROUPS, centre)
+            when(j - 1, GROUPS, add_bias)
+            when(j - 4, GROUPS, finish)
+            when(j - 2, GROUPS, residual)
+            when(j, UNITS, value_product)
+            when(j + 2, UNITS, transpose_attn)
             when(j + 2, UNITS, evacuate_attn)
-            when(j + 2, UNITS, regroup_pz_scalar)
-            when(j + 1, UNITS, value_product)
-            when(j + 3, UNITS, transpose_attn)
             if j == -2:
                 broadcast_vectors()
-            when(j + 1, GROUPS, add_bias)
+            when(j, UNITS, quantise_cat)
+            when(j - 1, GROUPS, project)
+            when(j + 1, UNITS, quantise_front)
+            when(j + 2, UNITS, regroup_pz_gpsimd)
+            when(j + 2, UNITS, regroup_pz_scalar)
+            when(j + 1, M, prepare_wo)
+            when(j - 2, GROUPS, deviations)

@@ -84,7 +84,7 @@ def tile_softmaxattention_pb_t_kernel(tc, attn, pz, Wo, bo, x, gamma, beta, out)
             return src, dst
 
         def regroup_pz_gpsimd(u):
-            pz_grouped[u] = grouped.tile([P, D, PACK], BF16, name="pz_grouped", align_bytes=64)
+            pz_grouped[u] = grouped.tile([P, D, PACK], BF16, name="pz_grouped", align_bytes=64, bufs=2)
             step = PZ_GROUPS_GPSIMD * 4 // PZ_PIECES
             for c0 in range(0, PZ_GROUPS_GPSIMD * 4, step):
                 nc.gpsimd.tensor_scalar(
@@ -280,6 +280,7 @@ def tile_softmaxattention_pb_t_kernel(tc, attn, pz, Wo, bo, x, gamma, beta, out)
             when(j + 4, UNITS, load_late_unit)
             if (j + 2) % 2 == 0:
                 when((j + 2) // 2, B, load_x)
+            when(j + 2, UNITS, regroup_pz_gpsimd)
             when(j - 3, GROUPS, centre)
             when(j - 1, GROUPS, add_bias)
             when(j - 4, GROUPS, finish)
@@ -292,7 +293,6 @@ def tile_softmaxattention_pb_t_kernel(tc, attn, pz, Wo, bo, x, gamma, beta, out)
             when(j, UNITS, quantise_cat)
             when(j - 1, GROUPS, project)
             when(j + 1, UNITS, quantise_front)
-            when(j + 2, UNITS, regroup_pz_gpsimd)
             when(j + 2, UNITS, regroup_pz_scalar)
             when(j + 1, M, prepare_wo)
             when(j - 2, GROUPS, deviations)

@@ -22,7 +22,7 @@ LN_EPS = 1e-5
 
 FLOPS = 2 * B * M * T * T * D + 2 * B * T * (M * D) * D
 
-PZ_GROUPS_GPSIMD = 80
+PZ_GROUPS_GPSIMD = 64
 PZ_PIECES = 2
 
 

@@ -22,8 +22,8 @@ LN_EPS = 1e-5
 
 FLOPS = 2 * B * M * T * T * D + 2 * B * T * (M * D) * D
 
-PZ_GROUPS_GPSIMD = 64
-PZ_PIECES = 2
+PZ_GROUPS_GPSIMD = 32
+PZ_GROUPS_VECTOR = 40
 
 
 def tile_softmaxattention_pb_t_kernel(tc, attn, pz, Wo, bo, x, gamma, beta, out):
@@ -85,20 +85,25 @@ def tile_softmaxattention_pb_t_kernel(tc, attn, pz, Wo, bo, x, gamma, beta, out)
 
         def regroup_pz_gpsimd(u):
             pz_grouped[u] = grouped.tile([P, D, PACK], BF16, name="pz_grouped", align_bytes=64, bufs=2)
-            step = PZ_GROUPS_GPSIMD * 4 // PZ_PIECES
-            for c0 in range(0, PZ_GROUPS_GPSIMD * 4, step):
-                nc.gpsimd.tensor_scalar(
-                    out=pz_grouped[u][:, c0 : c0 + step, :],
-                    in0=pz_sb[u][:, :, c0 : c0 + step].rearrange("p j i -> p i j"),
-                    scalar1=1.0,
-                    scalar2=0.0,
-                    op0=ALU.mult,
-                    op1=ALU.add,
-                )
+            columns = PZ_GROUPS_GPSIMD * 4
+            nc.gpsimd.tensor_scalar(
+                out=pz_grouped[u][:, :columns, :],
+                in0=pz_sb[u][:, :, :columns].rearrange("p j i -> p i j"),
+                scalar1=1.0,
+                scalar2=0.0,
+                op0=ALU.mult,
+                op1=ALU.add,
+            )
+
+        def regroup_pz_vector(u):
+            src, dst = pz_views(u)
+            g0, g1 = PZ_GROUPS_GPSIMD, PZ_GROUPS_GPSIMD + PZ_GROUPS_VECTOR
+            nc.vector.tensor_copy(out=dst[:, g0:g1], in_=src[:, g0:g1])
 
         def regroup_pz_scalar(u):
             src, dst = pz_views(u)
-            nc.scalar.copy(out=dst[:, PZ_GROUPS_GPSIMD:], in_=src[:, PZ_GROUPS_GPSIMD:])
+            g1 = PZ_GROUPS_GPSIMD + PZ_GROUPS_VECTOR
+            nc.scalar.copy(out=dst[:, g1:], in_=src[:, g1:])
 
         def quantise(name, values, bufs):
             n = values.shape[1] // PACK
@@ -293,6 +298,7 @@ def tile_softmaxattention_pb_t_kernel(tc, attn, pz, Wo, bo, x, gamma, beta, out)
             when(j, UNITS, quantise_cat)
             when(j - 1, GROUPS, project)
             when(j + 1, UNITS, quantise_front)
+            when(j + 2, UNITS, regroup_pz_vector)
             when(j + 2, UNITS, regroup_pz_scalar)
             when(j + 1, M, prepare_wo)
             when(j - 2, GROUPS, deviations)

@@ -22,8 +22,8 @@ LN_EPS = 1e-5
 
 FLOPS = 2 * B * M * T * T * D + 2 * B * T * (M * D) * D
 
-PZ_GROUPS_GPSIMD = 32
-PZ_GROUPS_VECTOR = 40
+PZ_GROUPS_GPSIMD = 52
+PZ_GROUPS_VECTOR = 24
 
 
 def tile_softmaxattention_pb_t_kernel(tc, attn, pz, Wo, bo, x, gamma, beta, out):

from contextlib import ExitStack

import concourse.mybir as mybir
from concourse.masks import make_identity

F32 = mybir.dt.float32
BF16 = mybir.dt.bfloat16
U32 = mybir.dt.uint32
U8 = mybir.dt.uint8
FP8X4 = mybir.dt.float8_e4m3fn_x4
ALU = mybir.AluOpType
ACT = mybir.ActivationFunctionType

P = 128
PACK = 4
B, M, T, D = 8, 2, 512, 512
R = T // P
UNITS = B * M
PAIR = 2
GROUPS = B * R // PAIR
LN_EPS = 1e-5

FLOPS = 2 * B * M * T * T * D + 2 * B * T * (M * D) * D

PZ_GROUPS_GPSIMD = 52
PZ_GROUPS_VECTOR = 24


def tile_softmaxattention_pb_t_kernel(tc, attn, pz, Wo, bo, x, gamma, beta, out):
    nc = tc.nc
    with ExitStack() as stack:
        consts = stack.enter_context(tc.tile_pool(name="consts", bufs=1))
        loads = stack.enter_context(tc.tile_pool(name="loads", bufs=5))
        grouped = stack.enter_context(tc.tile_pool(name="grouped", bufs=3))
        mx = stack.enter_context(tc.tile_pool(name="mx", bufs=2))
        rows = stack.enter_context(tc.tile_pool(name="rows", bufs=4))
        stats = stack.enter_context(tc.tile_pool(name="stats", bufs=8))
        psum_t = stack.enter_context(tc.psum_pool(name="psum_t", bufs=2))
        psum_cat = stack.enter_context(tc.psum_pool(name="psum_cat", bufs=3))
        psum_y = stack.enter_context(tc.psum_pool(name="psum_y", bufs=2))
        psum_consts = stack.enter_context(tc.psum_pool(name="psum_consts", bufs=1))
        stack.enter_context(tc.manual_schedule())

        attn_sb, pz_sb, x_sb = {}, {}, {}
        t_banks, attn_grouped, pz_grouped, cat_grouped = {}, {}, {}, {}
        attn_mx, pz_mx, cat_mx = {}, {}, {}
        h, scaled, row_sum, neg_mean, rstd, y_banks = {}, {}, {}, {}, {}, {}

        def load_unit(u):
            b, m = divmod(u, M)
            attn_sb[u] = loads.tile([P, R * T], BF16, name="attn_sb")
            nc.sync.dma_start(out=attn_sb[u][:], in_=attn[b, m].rearrange("(p r) s -> p (r s)", r=R))
            pz_sb[u] = loads.tile([P, PACK, D], BF16, name="pz_sb", bufs=5)
            nc.sync.dma_start(
                out=pz_sb[u][:].rearrange("p (v e) i -> p v (e i)", v=2),
                in_=pz[b, m].rearrange("(v p e) i -> p v (e i)", v=2, e=2),
            )

        def load_x(b):
            x_sb[b] = loads.tile([P, R, D], BF16, name="x_sb", bufs=3)
            nc.sync.dma_start(out=x_sb[b][:], in_=x[b].rearrange("(p r) o -> p r o", r=R))

        def transpose_attn(u):
            words = attn_sb[u][:].bitcast(F32).rearrange("p (r v w) -> p r v w", r=R, v=2)
            t_banks[u] = []
            for r0 in range(0, R, PAIR):
                t_bank = psum_t.tile([P, PAIR, 2, P], F32, name="t_bank")
                for r in range(PAIR):
                    for v in range(2):
                        nc.tensor.transpose(t_bank[:, r, v, :], words[:, r0 + r, v, :], ident_f32[:])
                t_banks[u].append(t_bank)

        def evacuate_attn(u):
            attn_grouped[u] = grouped.tile([P, R * P * PACK], BF16, name="attn_grouped", align_bytes=64)
            pairs = attn_grouped[u][:].bitcast(F32).rearrange("p (r t v) -> p r t v", r=R, v=2)
            for k, t_bank in enumerate(t_banks[u]):
                nc.scalar.copy(
                    out=pairs[:, k * PAIR : (k + 1) * PAIR], in_=t_bank[:].rearrange("p r v t -> p r t v")
                )

        def pz_views(u):
            src = pz_sb[u][:].rearrange("p j (g q) -> p g j q", q=4)
            dst = pz_grouped[u][:].rearrange("p (g q) j -> p g j q", q=4)
            return src, dst

        def regroup_pz_gpsimd(u):
            pz_grouped[u] = grouped.tile([P, D, PACK], BF16, name="pz_grouped", align_bytes=64, bufs=2)
            columns = PZ_GROUPS_GPSIMD * 4
            nc.gpsimd.tensor_scalar(
                out=pz_grouped[u][:, :columns, :],
                in0=pz_sb[u][:, :, :columns].rearrange("p j i -> p i j"),
                scalar1=1.0,
                scalar2=0.0,
                op0=ALU.mult,
                op1=ALU.add,
            )

        def regroup_pz_vector(u):
            src, dst = pz_views(u)
            g0, g1 = PZ_GROUPS_GPSIMD, PZ_GROUPS_GPSIMD + PZ_GROUPS_VECTOR
            nc.vector.tensor_copy(out=dst[:, g0:g1], in_=src[:, g0:g1])

        def regroup_pz_scalar(u):
            src, dst = pz_views(u)
            g1 = PZ_GROUPS_GPSIMD + PZ_GROUPS_VECTOR
            nc.scalar.copy(out=dst[:, g1:], in_=src[:, g1:])

        def quantise(name, values, bufs):
            n = values.shape[1] // PACK
            codes = mx.tile([P, n], U32, name=name + "_codes", align_bytes=64, bufs=bufs)
            scales = mx.tile([P, n], U8, name=name + "_scales", align_bytes=64, bufs=bufs)
            nc.vector.quantize_mx(out=codes[:].bitcast(FP8X4), scales=scales[:], in_=values)
            return codes, scales

        def quantise_front(u):
            attn_mx[u] = quantise("attn", attn_grouped[u][:], 2)
            pz_mx[u] = quantise("pz", pz_grouped[u][:].rearrange("p i j -> p (i j)"), 2)

        def value_product(u):
            attn_codes, attn_scales = attn_mx[u]
            pz_codes, pz_scales = pz_mx[u]
            cat_grouped[u] = grouped.tile([P, R, P, PACK], BF16, name="cat_grouped", align_bytes=64)
            for r in range(R):
                cat_bank = psum_cat.tile([P, PACK, P], F32, name="cat_bank")
                for c in range(PACK):
                    nc.tensor.matmul_mx(
                        out=cat_bank[:, c, :],
                        lhsT=pz_codes[:, c * P : (c + 1) * P].bitcast(FP8X4),
                        lhsT_scale=pz_scales[:, c * P : (c + 1) * P],
                        rhs=attn_codes[:, r * P : (r + 1) * P].bitcast(FP8X4),
                        rhs_scale=attn_scales[:, r * P : (r + 1) * P],
                        start=True,
                        stop=True,
                    )
                nc.scalar.copy(out=cat_grouped[u][:, r], in_=cat_bank[:].rearrange("p c t -> p t c"))

        def quantise_cat(u):
            cat_mx[u] = quantise("cat", cat_grouped[u][:].rearrange("p r t c -> p (r t c)"), 4)

        def add_bias(g):
            b, k = divmod(g, R // PAIR)
            for i in range(PAIR):
                h[g, i] = rows.tile([P, D], F32, name="h", bufs=2 * PAIR)
                nc.gpsimd.tensor_tensor(out=h[g, i][:], in0=x_sb[b][:, k * PAIR + i, :], in1=bo_all[:], op=ALU.add)

        def project(g):
            b, k = divmod(g, R // PAIR)
            for i in range(PAIR):
                r = k * PAIR + i
                y_banks[g, i] = psum_y.tile([P, D], F32, name="y_bank")
                for m in range(M):
                    cat_codes, cat_scales = cat_mx[b * M + m]
                    nc.tensor.matmul_mx(
                        out=y_banks[g, i][:],
                        lhsT=cat_codes[:, r * P : (r + 1) * P].bitcast(FP8X4),
                        lhsT_scale=cat_scales[:, r * P : (r + 1) * P],
                        rhs=wo_codes[:, m * D : (m + 1) * D].bitcast(FP8X4),
                        rhs_scale=wo_scales[:, m * D : (m + 1) * D],
                        start=(m == 0),
                        stop=(m == M - 1),
                    )

        def residual(g):
            row_sum[g] = stats.tile([P, PAIR], F32, name="row_sum")
            for i in range(PAIR):
                nc.vector.scalar_tensor_tensor(
                    out=h[g, i][:],
                    in0=y_banks[g, i][:],
                    scalar=1.0,
                    in1=h[g, i][:],
                    op0=ALU.mult,
                    op1=ALU.add,
                    accum_out=row_sum[g][:, i : i + 1],
                )

        def deviations(g):
            neg_mean[g] = stats.tile([P, PAIR], F32, name="neg_mean")
            nc.scalar.activation(out=neg_mean[g][:], in_=row_sum[g][:], func=ACT.Copy, scale=-1.0 / D)
            squares = rows.tile([P, PAIR, D], BF16, name="squares", bufs=2)
            dev_sum = stats.tile([P, PAIR], F32, name="dev_sum")
            for i in range(PAIR):
                nc.scalar.activation(
                    out=squares[:, i, :],
                    in_=h[g, i][:],
                    func=ACT.Square,
                    bias=neg_mean[g][:, i : i + 1],
                    scale=1.0,
                    accum_out=dev_sum[:, i : i + 1],
                )
            rstd[g] = stats.tile([P, PAIR], F32, name="rstd")
            nc.scalar.activation(
                out=rstd[g][:], in_=dev_sum[:], func=ACT.Abs_reciprocal_sqrt, bias=eps[:], scale=1.0 / D
            )

        def centre(g):
            scaled[g] = rows.tile([P, PAIR, D], F32, name="scaled", bufs=4)
            for i in range(PAIR):
                nc.vector.scalar_tensor_tensor(
                    out=scaled[g][:, i, :],
                    in0=h[g, i][:],
                    scalar=neg_mean[g][:, i : i + 1],
                    in1=gamma_all,
                    op0=ALU.add,
                    op1=ALU.mult,
                )

        def finish(g):
            b, k = divmod(g, R // PAIR)
            for i in range(PAIR):
                nc.vector.scalar_tensor_tensor(
                    out=scaled[g][:, i, :],
                    in0=scaled[g][:, i, :],
                    scalar=rstd[g][:, i : i + 1],
                    in1=beta_all,
                    op0=ALU.mult,
                    op1=ALU.add,
                )
            nc.sync.dma_start(
                out=out[b].rearrange("(p r) o -> p r o", r=R)[:, k * PAIR : (k + 1) * PAIR, :], in_=scaled[g][:]
            )

        def load_wo():
            nc.sync.dma_start(out=wo_sb[:], in_=Wo.rearrange("(a q) j -> q a j", q=P))

        def prepare_wo(m):
            for a0 in range(0, D // P, 2):
                wo_bank = psum_y.tile([P, 2, PACK, P], BF16, name="wo_bank", tag="y_bank")
                for a in range(2):
                    for c in range(PACK):
                        j0 = m * D + c * P
                        nc.tensor.transpose(wo_bank[:, a, c, :], wo_sb[:, a0 + a, j0 : j0 + P], ident_bf16[:])
                nc.vector.tensor_copy(
                    out=wo_grouped[:, m, a0 * P : (a0 + 2) * P, :].rearrange("p (a o) c -> p a o c", a=2),
                    in_=wo_bank[:].rearrange("p a c o -> p a o c"),
                )
            nc.vector.quantize_mx(
                out=wo_codes[:, m * D : (m + 1) * D].bitcast(FP8X4),
                scales=wo_scales[:, m * D : (m + 1) * D],
                in_=wo_grouped[:, m].rearrange("p o c -> p (o c)"),
            )

        def load_late_unit(u):
            if u >= 2:
                load_unit(u)

        def when(k, count, phase):
            if 0 <= k < count:
                phase(k)

        load_unit(0)
        load_unit(1)
        wo_sb = consts.tile([P, D // P, M * D], BF16, name="wo_sb")
        load_wo()
        wo_grouped = consts.tile([P, M, D, PACK], BF16, name="wo_grouped", align_bytes=64)
        wo_codes = consts.tile([P, M * D], U32, name="wo_codes", align_bytes=64)
        wo_scales = consts.tile([P, M * D], U8, name="wo_scales", align_bytes=64)

        ident_f32 = consts.tile([P, P], F32, name="ident_f32")
        make_identity(nc, ident_f32[:])
        ident_bf16 = consts.tile([P, P], BF16, name="ident_bf16")
        make_identity(nc, ident_bf16[:])
        eps = consts.tile([P, 1], F32, name="eps")
        nc.vector.memset(eps[:], LN_EPS)

        ones = consts.tile([P, P], BF16, name="ones")
        nc.vector.memset(ones[:], 1.0)
        vec_rows = consts.tile([P, 3, D], BF16, name="vec_rows")
        nc.vector.memset(vec_rows[:], 0.0)
        for v, vec in enumerate((bo, gamma, beta)):
            nc.scalar.dma_start(out=vec_rows[0:1, v, :], in_=vec.rearrange("(one d) -> one d", one=1))
        bo_all = consts.tile([P, D], F32, name="bo_all")
        affine_bank = psum_consts.tile([P, 2, D], BF16, name="affine_bank")
        gamma_all, beta_all = affine_bank[:, 0, :], affine_bank[:, 1, :]

        def broadcast_vectors():
            bo_bank = psum_y.tile([P, D], F32, name="bo_bank", tag="y_bank")
            nc.tensor.matmul(out=bo_bank[:], lhsT=ones[:], rhs=vec_rows[:, 0, :], start=True, stop=True)
            nc.vector.tensor_copy(out=bo_all[:], in_=bo_bank[:])
            for v in range(2):
                nc.tensor.matmul(
                    out=affine_bank[:, v, :], lhsT=ones[:], rhs=vec_rows[:, 1 + v, :], start=True, stop=True
                )

        for j in range(-2, GROUPS + 5):
            when(j + 4, UNITS, load_late_unit)
            if (j + 2) % 2 == 0:
                when((j + 2) // 2, B, load_x)
            when(j + 2, UNITS, regroup_pz_gpsimd)
            when(j - 3, GROUPS, centre)
            when(j - 1, GROUPS, add_bias)
            when(j - 4, GROUPS, finish)
            when(j - 2, GROUPS, residual)
            when(j, UNITS, value_product)
            when(j + 2, UNITS, transpose_attn)
            when(j + 2, UNITS, evacuate_attn)
            if j == -2:
                broadcast_vectors()
            when(j, UNITS, quantise_cat)
            when(j - 1, GROUPS, project)
            when(j + 1, UNITS, quantise_front)
            when(j + 2, UNITS, regroup_pz_vector)
            when(j + 2, UNITS, regroup_pz_scalar)
            when(j + 1, M, prepare_wo)
            when(j - 2, GROUPS, deviations)
